import numpy as np
import ml_dtypes


def mxq(x, axis, fmt="e4m3"):
    dtype, down = {"e4m3": (ml_dtypes.float8_e4m3fn, 7), "e5m2": (ml_dtypes.float8_e5m2, 14)}[fmt]
    v = np.moveaxis(np.asarray(x, np.float32).astype(ml_dtypes.bfloat16).astype(np.float64), axis, -1)
    blocks = v.reshape(v.shape[:-1] + (-1, 32))
    amax = np.abs(blocks).max(-1, keepdims=True)
    byte = np.maximum(np.where(amax > 0, np.frexp(amax)[1] - 1 + 127, 0) - down, 1)
    scale = np.exp2(byte - 127.0)
    codes = (blocks / scale).astype(np.float32).astype(dtype).astype(np.float64)
    return np.moveaxis((codes * scale).reshape(v.shape), -1, axis)


WIDE = False


def mx_kscale(k):
    if not WIDE:
        return np.ones(k)
    levels = np.array([10, -10, 5, -5, 0])
    if k % 512:
        return np.exp2(np.random.permutation(np.resize(levels, k // 32))).repeat(32)
    a = np.empty((k // 512, 16))
    for p in range(k // 512):
        a[p, :8] = np.random.permutation(np.resize(levels, 8))
        for g in range(8):
            far = levels[np.abs(levels - a[p, g]) >= 10]
            a[p, g + 8] = far[np.random.randint(len(far))]
    return np.exp2(a.ravel()).repeat(32)


BF16 = ml_dtypes.bfloat16


def bf(x):
    return np.asarray(x, np.float32).astype(BF16)


def f64(x):
    return np.asarray(x).astype(np.float64)


B, N, F, DIM, H, DH, D3 = 2, 64, 32, 2048, 12, 64, 512
W = H * D3
SCALE = 1.0 / (np.sqrt(DH) * H)
QS = np.sqrt(1.5 / (SCALE * np.sqrt(D3)))


def setup_inputs():
    s, t = mx_kscale(DIM), mx_kscale(D3)
    th = np.tile(t, H)
    return {"x": bf(np.random.standard_normal((B, N * F, DIM)) * s),
            "Wq": bf(np.random.standard_normal((DIM, W)) * QS / np.sqrt(DIM) / s[:, None] * th),
            "bq": bf(np.random.standard_normal(W) * 0.2 * QS * th),
            "k": bf(np.random.standard_normal((B, H, N, F, D3)) * QS / t)}


def reference(x, Wq, bq, k):
    y = (mxq(f64(x), 2, "e4m3") @ mxq(f64(Wq), 0, "e4m3")) + f64(bq)
    q = y.reshape(B, F, N, H, D3).transpose(0, 3, 2, 1, 4)
    s = (mxq(q, 4, "e4m3") @ mxq(f64(k), 4, "e4m3").transpose(0, 1, 2, 4, 3)) * SCALE
    e = np.exp(s - s.max(-1, keepdims=True))
    return e / e.sum(-1, keepdims=True)

@@ -1,0 +1,422 @@
+from contextlib import ExitStack
+
+import concourse.mybir as mybir
+from concourse.masks import make_identity
+
+F32 = mybir.dt.float32
+BF16 = mybir.dt.bfloat16
+U32 = mybir.dt.uint32
+U8 = mybir.dt.uint8
+FP8X4 = mybir.dt.float8_e4m3fn_x4
+ACT = mybir.ActivationFunctionType
+ALU = mybir.AluOpType
+AXIS = mybir.AxisListType
+
+CLIPS, PATCHES, FRAMES, DIM, HEADS, FEAT = 2, 64, 32, 2048, 12, 512
+FLOPS = 2 * CLIPS * PATCHES * FRAMES * DIM * HEADS * FEAT + 2 * CLIPS * HEADS * PATCHES * FRAMES * FRAMES * FEAT
+
+P = 128
+PASSES = DIM // 512
+CHUNKS = 8
+SLOTS = HEADS * CHUNKS
+SCALE = 1.0 / 96.0
+W_SLOTS = (0, 3, 4, 7)
+W_SLOTS_FIRST = (2, 3, 4, 7)
+LAST = SLOTS // 4 - 1
+
+
+def tile_dividedspacetimeattention_pa_l_kernel(tc, x, Wq, bq, k, out):
+    nc = tc.nc
+    with ExitStack() as ctx:
+        keep = ctx.enter_context(tc.tile_pool(name="keep", bufs=1))
+        stage = ctx.enter_context(tc.tile_pool(name="stage", bufs=2))
+        psum = ctx.enter_context(tc.psum_pool(name="psum", bufs=1))
+
+        ident = keep.tile([P, P], F32, name="ident")
+        make_identity(nc, ident[:])
+
+        ctx.enter_context(tc.manual_schedule())
+
+        bias_bf = keep.tile([P, HEADS, 4], BF16, name="bias_bf")
+        bias = keep.tile([P, HEADS * 4], F32, name="bias")
+        warm_in = keep.tile([P, 1], F32, name="warm_in")
+        warm_out = keep.tile([P, 1], F32, name="warm_out")
+        x_codes = []
+        x_scales = []
+        for c in range(CHUNKS):
+            x_codes.append(keep.tile([P, PASSES, 512], U32, name="x_codes%d" % c, align_bytes=64))
+            x_scales.append(keep.tile([P, PASSES, 512], U8, name="x_scales%d" % c, align_bytes=64))
+
+        xraw, xsrt, xbanks, xgrp = {}, {}, {}, {}
+        kraw, ksrt, kbanks, kgrp, kcodes = {}, {}, {}, {}, {}
+        wraw, wgrp, wcodes = {}, {}, {}
+        qrows, qgrp, qcodes = {}, {}, {}
+        scores, probs = {}, {}
+
+        def sort_words(raw, tag):
+            srt = stage.tile([P, 1024], F32, tag=tag, bufs=2, name=tag)
+            nc.vector.tensor_copy(
+                out=srt[:].rearrange("p (a u w) -> p a u w", a=4, u=2),
+                in_=raw[:].bitcast(F32).rearrange("p (a w u) -> p a u w", a=4, u=2),
+            )
+            return srt
+
+        def turn(srt):
+            banks = []
+            for half in range(2):
+                bank = psum.tile([P, 4, P], F32, tag="tp", bufs=4, name="tp")
+                for q in range(4):
+                    lo = (4 * half + q) * P
+                    nc.tensor.transpose(bank[:, q, :], srt[:, lo : lo + P], ident[:])
+                banks.append(bank)
+            return banks
+
+        def load_x(c, i):
+            b, m = divmod(c, 4)
+            raw = stage.tile([P, DIM], BF16, tag="xraw", bufs=4, name="xraw")
+            nc.sync.dma_start(out=raw[:], in_=x[b, 4 * m + i : PATCHES * FRAMES : 16, :])
+            xraw[(c, i)] = raw
+
+        def sort_x(c, i):
+            xsrt[(c, i)] = sort_words(xraw.pop((c, i)), "xsrt")
+            if c + 1 < CHUNKS:
+                load_x(c + 1, i)
+
+        def turn_x(c, i):
+            xbanks[(c, i)] = turn(xsrt.pop((c, i)))
+
+        def out_x(c, i):
+            banks = xbanks.pop((c, i))
+            grp = stage.tile([P, 2048], BF16, tag="xgrp", bufs=3, name="xgrp", align_bytes=64)
+            words = grp[:].bitcast(F32).rearrange("p (g j f u) -> p g j f u", g=4, j=4, u=2)
+            for g in range(PASSES):
+                lo = 2 * (g % 2)
+                nc.scalar.copy(
+                    out=words[:, g, :, :, :],
+                    in_=banks[g // 2][:, lo : lo + 2, :].rearrange("p u (f j) -> p j f u", j=4),
+                )
+            xgrp[(c, i)] = grp
+
+        def quant_x(c, i):
+            grp = xgrp.pop((c, i))
+            for g in range(PASSES):
+                nc.vector.quantize_mx(
+                    out=x_codes[c][:, g, i * P : (i + 1) * P].bitcast(FP8X4),
+                    scales=x_scales[c][:, g, i * P : (i + 1) * P],
+                    in_=grp[:, g * 512 : (g + 1) * 512],
+                )
+
+        def load_w(h, g):
+            raw = stage.tile([P, 4, 512], BF16, tag="wraw", bufs=4, name="wraw")
+            nc.sync.dma_start(
+                out=raw[:],
+                in_=Wq[512 * g : 512 * (g + 1), 512 * h : 512 * (h + 1)].rearrange("(p j) c -> p j c", j=4),
+            )
+            wraw[(h, g)] = raw
+
+        def group_w(h, g, shared):
+            raw = wraw.pop((h, g))
+            grp = stage.tile([P, 2048], BF16, tag="wgrp", bufs=2, name="wgrp", align_bytes=64)
+            dst = grp[:].rearrange("p (t m j) -> p t m j", t=4, j=4)
+            src = raw[:].rearrange("p j (m t) -> p t m j", t=4)
+            if shared:
+                nc.vector.tensor_copy(out=dst[:, 0:2, :, :], in_=src[:, 0:2, :, :])
+                nc.scalar.copy(out=dst[:, 2:4, :, :], in_=src[:, 2:4, :, :])
+            else:
+                nc.vector.tensor_copy(out=dst, in_=src)
+            wgrp[(h, g)] = grp
+
+        def quant_w(h, g):
+            grp = wgrp.pop((h, g))
+            if g == 0:
+                wc = stage.tile([P, PASSES, 512], U32, tag="wc", bufs=2, name="wc", align_bytes=64)
+                ws = stage.tile([P, PASSES, 512], U8, tag="ws", bufs=2, name="ws", align_bytes=64)
+                wcodes[h] = (wc, ws)
+            wc, ws = wcodes[h]
+            nc.vector.quantize_mx(out=wc[:, g, :].bitcast(FP8X4), scales=ws[:, g, :], in_=grp[:])
+
+        def load_k(s):
+            h, c = divmod(s, CHUNKS)
+            b, m = divmod(c, 4)
+            raw = stage.tile([P, 2048], BF16, tag="kraw", bufs=4, name="kraw")
+            nc.sync.dma_start(
+                out=raw[:].rearrange("p (j d) -> p j d", j=4),
+                in_=k[b, h].rearrange("(j q) g d -> (q g) j d", j=4)[P * m : P * (m + 1), :, :],
+            )
+            kraw[s] = raw
+
+        def sort_k(s):
+            ksrt[s] = sort_words(kraw.pop(s), "ksrt")
+
+        def turn_k(s):
+            kbanks[s] = turn(ksrt.pop(s))
+
+        def out_k(s):
+            banks = kbanks.pop(s)
+            grp = stage.tile([P, 2048], BF16, tag="kgrp", bufs=2, name="kgrp", align_bytes=64)
+            words = grp[:].bitcast(F32).rearrange("p (i j g u) -> p i j g u", i=4, j=4, u=2)
+            for j in range(4):
+                lo = 2 * (j % 2)
+                nc.scalar.copy(
+                    out=words[:, :, j, :, :],
+                    in_=banks[j // 2][:, lo : lo + 2, :].rearrange("p u (i g) -> p i g u", i=4),
+                )
+            kgrp[s] = grp
+
+        def quant_k(s):
+            grp = kgrp.pop(s)
+            kc = stage.tile([P, 512], U32, tag="kc", bufs=3, name="kc", align_bytes=64)
+            ks = stage.tile([P, 512], U8, tag="ks", bufs=3, name="ks", align_bytes=64)
+            nc.vector.quantize_mx(out=kc[:].bitcast(FP8X4), scales=ks[:], in_=grp[:])
+            kcodes[s] = (kc, ks)
+
+        def project(s, t):
+            h, c = divmod(s, CHUNKS)
+            wc, ws = wcodes[h]
+            acc = psum.tile([P, 512], F32, tag="acc", bufs=3, name="acc")
+            for g in range(PASSES):
+                nc.tensor.matmul_mx(
+                    out=acc[:],
+                    lhsT=wc[:, g, t * P : (t + 1) * P].bitcast(FP8X4),
+                    lhsT_scale=ws[:, g, t * P : (t + 1) * P],
+                    rhs=x_codes[c][:, g, :].bitcast(FP8X4),
+                    rhs_scale=x_scales[c][:, g, :],
+                    start=(g == 0),
+                    stop=(g == PASSES - 1),
+                )
+            if t == 0:
+                qrows[s] = stage.tile([P, 4, 512], BF16, tag="qb", bufs=2, name="qb")
+            nc.scalar.activation(
+                out=qrows[s][:, t, :],
+                in_=acc[:],
+                func=ACT.Identity,
+                bias=bias[:, 4 * h + t : 4 * h + t + 1],
+                scale=1.0,
+            )
+
+        def group_q(s):
+            rows = qrows.pop(s)
+            grp = stage.tile([P, 2048], BF16, tag="qg", bufs=2, name="qg", align_bytes=64)
+            nc.vector.tensor_copy(
+                out=grp[:].rearrange("p (c t) -> p c t", t=4),
+                in_=rows[:].rearrange("p t c -> p c t"),
+            )
+            qgrp[s] = grp
+
+        def quant_q(s):
+            grp = qgrp.pop(s)
+            qc = stage.tile([P, 512], U32, tag="qc", bufs=2, name="qc", align_bytes=64)
+            qs = stage.tile([P, 512], U8, tag="qs", bufs=2, name="qs", align_bytes=64)
+            nc.vector.quantize_mx(out=qc[:].bitcast(FP8X4), scales=qs[:], in_=grp[:])
+            qcodes[s] = (qc, qs)
+
+        def score(s):
+            qc, qs = qcodes.pop(s)
+            kc, ks = kcodes.pop(s)
+            sc = psum.tile([P, 4, P], F32, tag="sc", bufs=1, name="sc")
+            for i in range(4):
+                nc.tensor.matmul_mx(
+                    out=sc[:, i, :],
+                    lhsT=qc[:, i * P : (i + 1) * P].bitcast(FP8X4),
+                    lhsT_scale=qs[:, i * P : (i + 1) * P],
+                    rhs=kc[:, i * P : (i + 1) * P].bitcast(FP8X4),
+                    rhs_scale=ks[:, i * P : (i + 1) * P],
+                    start=True,
+                    stop=True,
+                )
+            grp, m = divmod(s, 4)
+            if m == 0:
+                scores[grp] = stage.tile([P, 16, FRAMES], F32, tag="cmp", bufs=2, name="cmp")
+            for j in range(4):
+                lo = 32 * j
+                nc.scalar.copy(
+                    out=scores[grp][lo : lo + 32, 4 * m : 4 * m + 4, :],
+                    in_=sc[lo : lo + 32, :, lo : lo + 32],
+                )
+
+        stats = {}
+
+        def soft_max(grp, lo, hi):
+            mx = stage.tile([P, 16], F32, tag="mx", bufs=2, name="mx")
+            nc.vector.tensor_reduce(out=mx[:, lo:hi], in_=scores[grp][:, lo:hi, :], axis=AXIS.X, op=ALU.max)
+            stats[(grp, lo)] = mx
+
+        def soft_sub(grp, lo, hi):
+            mx = stats.pop((grp, lo))
+            nc.vector.tensor_tensor(
+                out=scores[grp][:, lo:hi, :],
+                in0=scores[grp][:, lo:hi, :],
+                in1=mx[:, lo:hi].unsqueeze(2).to_broadcast([P, hi - lo, FRAMES]),
+                op=ALU.subtract,
+            )
+
+        def soft_exp(grp, lo, hi):
+            if lo == 0:
+                probs[grp] = stage.tile([P, 16, FRAMES], F32, tag="ex", bufs=2, name="ex")
+            nc.scalar.activation(out=probs[grp][:, lo:hi, :], in_=scores[grp][:, lo:hi, :], func=ACT.Exp, scale=SCALE)
+
+        def soft_sum(grp, lo, hi):
+            sm = stage.tile([P, 16], F32, tag="sm", bufs=2, name="sm")
+            nc.vector.tensor_reduce(out=sm[:, lo:hi], in_=probs[grp][:, lo:hi, :], axis=AXIS.X, op=ALU.add)
+            stats[(grp, lo)] = sm
+
+        def soft_recip(grp, lo, hi):
+            rs = stage.tile([P, 16], F32, tag="rs", bufs=2, name="rs")
+            nc.vector.reciprocal(out=rs[:, lo:hi], in_=stats.pop((grp, lo))[:, lo:hi])
+            stats[(grp, lo)] = rs
+
+        def soft_mul(grp, lo, hi):
+            rs = stats.pop((grp, lo))
+            nc.vector.tensor_tensor(
+                out=probs[grp][:, lo:hi, :],
+                in0=probs[grp][:, lo:hi, :],
+                in1=rs[:, lo:hi].unsqueeze(2).to_broadcast([P, hi - lo, FRAMES]),
+                op=ALU.mult,
+            )
+
+        def store(grp, lo, hi):
+            h, b = divmod(grp, CLIPS)
+            view = out[b, h].rearrange("(j q) f g -> j f q g", j=4)
+            for j in range(4):
+                nc.sync.dma_start(out=view[j][:, lo:hi, :], in_=probs[grp][32 * j : 32 * j + 32, lo:hi, :])
+
+        nc.vector.memset(warm_in[:], 0.0)
+        nc.scalar.activation(out=warm_out[:], in_=warm_in[:], func=ACT.Exp)
+        load_x(0, 0)
+        load_x(0, 1)
+        load_w(0, 0)
+        load_x(0, 2)
+        load_w(0, 1)
+        load_x(0, 3)
+        load_w(0, 2)
+        load_w(0, 3)
+        nc.sync.dma_start(out=bias_bf[:], in_=bq.rearrange("(h p t) -> p h t", h=HEADS, t=4))
+
+        sort_x(0, 0)
+        turn_x(0, 0)
+        sort_x(0, 1)
+        out_x(0, 0)
+        turn_x(0, 1)
+        group_w(0, 0, True)
+        quant_x(0, 0)
+        sort_x(0, 2)
+        out_x(0, 1)
+        turn_x(0, 2)
+        quant_w(0, 0)
+        group_w(0, 1, True)
+        quant_x(0, 1)
+        sort_x(0, 3)
+        for s in range(3):
+            load_k(s)
+        out_x(0, 2)
+        turn_x(0, 3)
+        quant_w(0, 1)
+        group_w(0, 2, True)
+        quant_x(0, 2)
+        out_x(0, 3)
+        quant_w(0, 2)
+        group_w(0, 3, True)
+        quant_x(0, 3)
+        quant_w(0, 3)
+        nc.vector.tensor_copy(out=bias[:], in_=bias_bf[:].rearrange("p h t -> p (h t)"))
+        sort_x(1, 0)
+        sort_x(1, 1)
+
+        for it in range(SLOTS + 1):
+            h, c = divmod(it, CHUNKS)
+            live = it < SLOTS
+            fresh = it + 1 if it + 1 < CHUNKS else None
+
+            if it + 3 < SLOTS:
+                load_k(it + 3)
+            for g in range(PASSES):
+                hn = (it + 2) // CHUNKS
+                for hh in (hn - 1, hn):
+                    if 0 <= hh < HEADS - 1 and CHUNKS * hh + (W_SLOTS_FIRST if hh == 0 else W_SLOTS)[g] == it + 2:
+                        load_w(hh + 1, g)
+            if it % 4 == 3 and it >= 7:
+                store((it - 7) // 4, 0, 16)
+
+            ks_now = [0, 1] if it == 1 else ([it] if 2 <= it < SLOTS else [])
+            for s in ks_now:
+                out_k(s)
+            if 1 <= it <= SLOTS:
+                group_q(it - 1)
+            if it == SLOTS:
+                soft_max(LAST, 0, 12)
+            if it % 4 == 1 and it >= 5:
+                soft_max((it - 5) // 4, 0, 16)
+            if it % 4 == 2 and it >= 6:
+                soft_sum((it - 6) // 4, 0, 16)
+            for s in ks_now:
+                quant_k(s)
+            if it % 4 == 2 and it >= 6:
+                soft_recip((it - 6) // 4, 0, 16)
+            if 1 <= it <= SLOTS:
+                quant_q(it - 1)
+            if it == SLOTS:
+                soft_sub(LAST, 0, 12)
+                soft_exp(LAST, 0, 12)
+            if it % 4 == 1 and it >= 5:
+                soft_sub((it - 5) // 4, 0, 16)
+            if it % 4 == 2 and it >= 6:
+                soft_mul((it - 6) // 4, 0, 16)
+
+            w_now = None
+            w_slots = W_SLOTS_FIRST if h == 0 else W_SLOTS
+            if live and h + 1 < HEADS and c in w_slots:
+                w_now = (h + 1, w_slots.index(c))
+
+            if live:
+                for t in range(4):
+                    project(it, t)
+                    if fresh is not None:
+                        turn_x(fresh, t)
+                        out_x(fresh, t)
+                        if t < 2:
+                            sort_x(fresh, t + 2)
+                        if t > 0:
+                            quant_x(fresh, t - 1)
+                    if t == 0 and w_now is not None:
+                        group_w(w_now[0], w_now[1], False)
+                    if t == 2 and it % 4 == 1 and it >= 5:
+                        soft_exp((it - 5) // 4, 0, 16)
+
+            if it == 0:
+                sort_k(0)
+                sort_k(1)
+            elif it + 2 < SLOTS:
+                sort_k(it + 2)
+            if w_now is not None:
+                quant_w(w_now[0], w_now[1])
+
+            if 1 <= it <= SLOTS:
+                score(it - 1)
+            if it == 0:
+                turn_k(0)
+                turn_k(1)
+                sort_k(2)
+            elif it < CHUNKS - 1:
+                turn_k(it + 1)
+            elif it % 2 == 1:
+                for s in (it + 1, it + 2):
+                    if s < SLOTS:
+                        turn_k(s)
+
+            if fresh is not None:
+                quant_x(fresh, 3)
+                if fresh + 1 < CHUNKS:
+                    sort_x(fresh + 1, 0)
+                    sort_x(fresh + 1, 1)
+
+        soft_sum(LAST, 0, 12)
+        soft_max(LAST, 12, 16)
+        soft_recip(LAST, 0, 12)
+        soft_sub(LAST, 12, 16)
+        soft_mul(LAST, 0, 12)
+        soft_exp(LAST, 12, 16)
+        store(LAST, 0, 12)
+        soft_sum(LAST, 12, 16)
+        soft_recip(LAST, 12, 16)
+        soft_mul(LAST, 12, 16)
+        store(LAST, 12, 16)

@@ -20,8 +20,8 @@ PASSES = DIM // 512
 CHUNKS = 8
 SLOTS = HEADS * CHUNKS
 SCALE = 1.0 / 96.0
-W_SLOTS = (0, 3, 4, 7)
-W_SLOTS_FIRST = (2, 3, 4, 7)
+W_SLOTS = (0, 2, 4, 6)
+W_SLOTS_FIRST = (1, 3, 4, 6)
 LAST = SLOTS // 4 - 1
 
 
@@ -54,7 +54,7 @@ def tile_dividedspacetimeattention_pa_l_kernel(tc, x, Wq, bq, k, out):
         scores, probs = {}, {}
 
         def sort_words(raw, tag):
-            srt = stage.tile([P, 1024], F32, tag=tag, bufs=2, name=tag)
+            srt = stage.tile([P, 1024], F32, tag=tag, bufs=(3 if tag == "ksrt" else 2), name=tag)
             nc.vector.tensor_copy(
                 out=srt[:].rearrange("p (a u w) -> p a u w", a=4, u=2),
                 in_=raw[:].bitcast(F32).rearrange("p (a w u) -> p a u w", a=4, u=2),
@@ -151,17 +151,18 @@ def tile_dividedspacetimeattention_pa_l_kernel(tc, x, Wq, bq, k, out):
         def turn_k(s):
             kbanks[s] = turn(ksrt.pop(s))
 
-        def out_k(s):
-            banks = kbanks.pop(s)
-            grp = stage.tile([P, 2048], BF16, tag="kgrp", bufs=2, name="kgrp", align_bytes=64)
-            words = grp[:].bitcast(F32).rearrange("p (i j g u) -> p i j g u", i=4, j=4, u=2)
-            for j in range(4):
-                lo = 2 * (j % 2)
+        def out_k(s, half):
+            if half == 0:
+                kgrp[s] = stage.tile([P, 2048], BF16, tag="kgrp", bufs=2, name="kgrp", align_bytes=64)
+            words = kgrp[s][:].bitcast(F32).rearrange("p (i j g u) -> p i j g u", i=4, j=4, u=2)
+            bank = kbanks[s][half]
+            for q in range(2):
                 nc.scalar.copy(
-                    out=words[:, :, j, :, :],
-                    in_=banks[j // 2][:, lo : lo + 2, :].rearrange("p u (i g) -> p i g u", i=4),
+                    out=words[:, :, 2 * half + q, :, :],
+                    in_=bank[:, 2 * q : 2 * q + 2, :].rearrange("p u (i g) -> p i g u", i=4),
                 )
-            kgrp[s] = grp
+            if half == 1:
+                kbanks.pop(s)
 
         def quant_k(s):
             grp = kgrp.pop(s)
@@ -224,6 +225,9 @@ def tile_dividedspacetimeattention_pa_l_kernel(tc, x, Wq, bq, k, out):
                     start=True,
                     stop=True,
                 )
+            return sc
+
+        def pick(s, sc):
             grp, m = divmod(s, 4)
             if m == 0:
                 scores[grp] = stage.tile([P, 16, FRAMES], F32, tag="cmp", bufs=2, name="cmp")
@@ -280,6 +284,18 @@ def tile_dividedspacetimeattention_pa_l_kernel(tc, x, Wq, bq, k, out):
             for j in range(4):
                 nc.sync.dma_start(out=view[j][:, lo:hi, :], in_=probs[grp][32 * j : 32 * j + 32, lo:hi, :])
 
+        k_sort_slot = []
+        for s in range(SLOTS):
+            if s < 3:
+                k_sort_slot.append(0)
+            elif s <= CHUNKS + 1:
+                k_sort_slot.append(s - 2)
+            elif s == CHUNKS + 2:
+                k_sort_slot.append(CHUNKS - 1)
+            else:
+                k_sort_slot.append(s - 3)
+        k_load_slot = [(1 if s == 4 else k_sort_slot[s] - 2) for s in range(SLOTS)]
+
         nc.vector.memset(warm_in[:], 0.0)
         nc.scalar.activation(out=warm_out[:], in_=warm_in[:], func=ACT.Exp)
         load_x(0, 0)
@@ -306,8 +322,12 @@ def tile_dividedspacetimeattention_pa_l_kernel(tc, x, Wq, bq, k, out):
         group_w(0, 1, True)
         quant_x(0, 1)
         sort_x(0, 3)
-        for s in range(3):
-            load_k(s)
+        for s in range(SLOTS):
+            if k_load_slot[s] < 0:
+                load_k(s)
+        for g in range(PASSES):
+            if W_SLOTS_FIRST[g] < 2:
+                load_w(1, g)
         out_x(0, 2)
         turn_x(0, 3)
         quant_w(0, 1)
@@ -325,47 +345,66 @@ def tile_dividedspacetimeattention_pa_l_kernel(tc, x, Wq, bq, k, out):
         for it in range(SLOTS + 1):
             h, c = divmod(it, CHUNKS)
             live = it < SLOTS
+            first = it < CHUNKS
             fresh = it + 1 if it + 1 < CHUNKS else None
+            w_slots = W_SLOTS_FIRST if h == 0 else W_SLOTS
 
-            if it + 3 < SLOTS:
-                load_k(it + 3)
-            for g in range(PASSES):
-                hn = (it + 2) // CHUNKS
-                for hh in (hn - 1, hn):
-                    if 0 <= hh < HEADS - 1 and CHUNKS * hh + (W_SLOTS_FIRST if hh == 0 else W_SLOTS)[g] == it + 2:
+            for s in range(SLOTS):
+                if k_load_slot[s] == it:
+                    load_k(s)
+            for hh in (h, h + 1):
+                for g in range(PASSES):
+                    if hh < HEADS - 1 and CHUNKS * hh + (W_SLOTS_FIRST if hh == 0 else W_SLOTS)[g] == it + 2:
                         load_w(hh + 1, g)
-            if it % 4 == 3 and it >= 7:
-                store((it - 7) // 4, 0, 16)
+            if it % 4 == 0 and it >= 8:
+                store((it - 8) // 4, 0, 16)
 
+            part_a = (it - 5) // 4 if (it % 4 == 1 and 5 <= it < SLOTS) else None
+            part_b = (it - 7) // 4 if (it % 4 == 3 and 7 <= it < SLOTS) else None
+            w_now = (h + 1, w_slots.index(c)) if (live and h + 1 < HEADS and c in w_slots) else None
+            sorts = [s for s in range(3, SLOTS) if k_sort_slot[s] == it]
             ks_now = [0, 1] if it == 1 else ([it] if 2 <= it < SLOTS else [])
-            for s in ks_now:
-                out_k(s)
-            if 1 <= it <= SLOTS:
+
+            if first:
+                for s in ks_now:
+                    out_k(s, 0)
+                    out_k(s, 1)
+            if 1 <= it:
                 group_q(it - 1)
-            if it == SLOTS:
+            if first:
+                for s in ks_now:
+                    quant_k(s)
+            elif part_a is not None:
+                soft_max(part_a, 0, 16)
+            elif part_b is not None:
+                soft_sum(part_b, 0, 16)
+            elif it == SLOTS:
                 soft_max(LAST, 0, 12)
-            if it % 4 == 1 and it >= 5:
-                soft_max((it - 5) // 4, 0, 16)
-            if it % 4 == 2 and it >= 6:
-                soft_sum((it - 6) // 4, 0, 16)
-            for s in ks_now:
-                quant_k(s)
-            if it % 4 == 2 and it >= 6:
-                soft_recip((it - 6) // 4, 0, 16)
-            if 1 <= it <= SLOTS:
+            else:
+                for s in sorts:
+                    sort_k(s)
+                sorts = []
+            if 1 <= it:
                 quant_q(it - 1)
+            if first and part_a is not None:
+                soft_max(part_a, 0, 16)
+            if first and part_b is not None:
+                soft_sum(part_b, 0, 16)
+            if part_b is not None:
+                soft_recip(part_b, 0, 16)
+            if not first:
+                for s in sorts:
+                    sort_k(s)
+                sorts = []
+            if part_a is not None:
+                soft_sub(part_a, 0, 16)
+            if part_b is not None:
+                soft_mul(part_b, 0, 16)
             if it == SLOTS:
                 soft_sub(LAST, 0, 12)
                 soft_exp(LAST, 0, 12)
-            if it % 4 == 1 and it >= 5:
-                soft_sub((it - 5) // 4, 0, 16)
-            if it % 4 == 2 and it >= 6:
-                soft_mul((it - 6) // 4, 0, 16)
-
-            w_now = None
-            w_slots = W_SLOTS_FIRST if h == 0 else W_SLOTS
-            if live and h + 1 < HEADS and c in w_slots:
-                w_now = (h + 1, w_slots.index(c))
+            if w_now is not None and not first:
+                group_w(w_now[0], w_now[1], False)
 
             if live:
                 for t in range(4):
@@ -377,21 +416,25 @@ def tile_dividedspacetimeattention_pa_l_kernel(tc, x, Wq, bq, k, out):
                             sort_x(fresh, t + 2)
                         if t > 0:
                             quant_x(fresh, t - 1)
-                    if t == 0 and w_now is not None:
+                    if t == 0 and w_now is not None and first:
                         group_w(w_now[0], w_now[1], False)
-                    if t == 2 and it % 4 == 1 and it >= 5:
-                        soft_exp((it - 5) // 4, 0, 16)
+                    if t < 2 and not first:
+                        out_k(it, t)
+                    if t == 3 and part_a is not None:
+                        soft_exp(part_a, 0, 16)
 
+            if not first and live:
+                quant_k(it)
             if it == 0:
                 sort_k(0)
                 sort_k(1)
-            elif it + 2 < SLOTS:
-                sort_k(it + 2)
+            for s in sorts:
+                sort_k(s)
             if w_now is not None:
                 quant_w(w_now[0], w_now[1])
 
-            if 1 <= it <= SLOTS:
-                score(it - 1)
+            if 1 <= it:
+                pick(it - 1, score(it - 1))
             if it == 0:
                 turn_k(0)
                 turn_k(1)

@@ -37,6 +37,12 @@ def tile_dividedspacetimeattention_pa_l_kernel(tc, x, Wq, bq, k, out):
 
         ctx.enter_context(tc.manual_schedule())
 
+        perm = keep.tile([P, P], F32, name="perm")
+        nc.vector.tensor_copy(
+            out=perm[:].rearrange("p (j f) -> p j f", j=4),
+            in_=ident[:].rearrange("p (f j) -> p j f", j=4),
+        )
+
         bias_bf = keep.tile([P, HEADS, 4], BF16, name="bias_bf")
         bias = keep.tile([P, HEADS * 4], F32, name="bias")
         warm_in = keep.tile([P, 1], F32, name="warm_in")
@@ -56,18 +62,18 @@ def tile_dividedspacetimeattention_pa_l_kernel(tc, x, Wq, bq, k, out):
         def sort_words(raw, tag):
             srt = stage.tile([P, 1024], F32, tag=tag, bufs=(3 if tag == "ksrt" else 2), name=tag)
             nc.vector.tensor_copy(
-                out=srt[:].rearrange("p (a u w) -> p a u w", a=4, u=2),
-                in_=raw[:].bitcast(F32).rearrange("p (a w u) -> p a u w", a=4, u=2),
+                out=srt[:].rearrange("p (a u w) -> p a w u", a=4, u=2),
+                in_=raw[:].bitcast(F32).rearrange("p (a w u) -> p a w u", a=4, u=2),
             )
             return srt
 
-        def turn(srt):
+        def turn(srt, order):
             banks = []
             for half in range(2):
                 bank = psum.tile([P, 4, P], F32, tag="tp", bufs=4, name="tp")
                 for q in range(4):
                     lo = (4 * half + q) * P
-                    nc.tensor.transpose(bank[:, q, :], srt[:, lo : lo + P], ident[:])
+                    nc.tensor.transpose(bank[:, q, :], srt[:, lo : lo + P], order[:])
                 banks.append(bank)
             return banks
 
@@ -83,17 +89,16 @@ def tile_dividedspacetimeattention_pa_l_kernel(tc, x, Wq, bq, k, out):
                 load_x(c + 1, i)
 
         def turn_x(c, i):
-            xbanks[(c, i)] = turn(xsrt.pop((c, i)))
+            xbanks[(c, i)] = turn(xsrt.pop((c, i)), perm)
 
         def out_x(c, i):
             banks = xbanks.pop((c, i))
             grp = stage.tile([P, 2048], BF16, tag="xgrp", bufs=3, name="xgrp", align_bytes=64)
-            words = grp[:].bitcast(F32).rearrange("p (g j f u) -> p g j f u", g=4, j=4, u=2)
-            for g in range(PASSES):
-                lo = 2 * (g % 2)
+            words = grp[:].bitcast(F32).rearrange("p (g r u) -> p g r u", g=4, u=2)
+            for half in range(2):
                 nc.scalar.copy(
-                    out=words[:, g, :, :, :],
-                    in_=banks[g // 2][:, lo : lo + 2, :].rearrange("p u (f j) -> p j f u", j=4),
+                    out=words[:, 2 * half : 2 * half + 2, :, :],
+                    in_=banks[half][:].rearrange("p (g u) r -> p g r u", u=2),
                 )
             xgrp[(c, i)] = grp
 
@@ -117,11 +122,11 @@ def tile_dividedspacetimeattention_pa_l_kernel(tc, x, Wq, bq, k, out):
         def group_w(h, g, shared):
             raw = wraw.pop((h, g))
             grp = stage.tile([P, 2048], BF16, tag="wgrp", bufs=2, name="wgrp", align_bytes=64)
-            dst = grp[:].rearrange("p (t m j) -> p t m j", t=4, j=4)
-            src = raw[:].rearrange("p j (m t) -> p t m j", t=4)
+            dst = grp[:].rearrange("p (t m j) -> p m t j", t=4, j=4)
+            src = raw[:].rearrange("p j (m t) -> p m t j", t=4)
             if shared:
-                nc.vector.tensor_copy(out=dst[:, 0:2, :, :], in_=src[:, 0:2, :, :])
-                nc.scalar.copy(out=dst[:, 2:4, :, :], in_=src[:, 2:4, :, :])
+                nc.vector.tensor_copy(out=dst[:, :, 0:2, :], in_=src[:, :, 0:2, :])
+                nc.scalar.copy(out=dst[:, :, 2:4, :], in_=src[:, :, 2:4, :])
             else:
                 nc.vector.tensor_copy(out=dst, in_=src)
             wgrp[(h, g)] = grp
@@ -149,7 +154,7 @@ def tile_dividedspacetimeattention_pa_l_kernel(tc, x, Wq, bq, k, out):
             ksrt[s] = sort_words(kraw.pop(s), "ksrt")
 
         def turn_k(s):
-            kbanks[s] = turn(ksrt.pop(s))
+            kbanks[s] = turn(ksrt.pop(s), ident)
 
         def out_k(s, half):
             if half == 0:
@@ -199,8 +204,8 @@ def tile_dividedspacetimeattention_pa_l_kernel(tc, x, Wq, bq, k, out):
             rows = qrows.pop(s)
             grp = stage.tile([P, 2048], BF16, tag="qg", bufs=2, name="qg", align_bytes=64)
             nc.vector.tensor_copy(
-                out=grp[:].rearrange("p (c t) -> p c t", t=4),
-                in_=rows[:].rearrange("p t c -> p c t"),
+                out=grp[:].rearrange("p (c i t) -> p c t i", i=4, t=4),
+                in_=rows[:].rearrange("p t (c i) -> p c t i", i=4),
             )
             qgrp[s] = grp
 

@@ -16,13 +16,18 @@ CLIPS, PATCHES, FRAMES, DIM, HEADS, FEAT = 2, 64, 32, 2048, 12, 512
 FLOPS = 2 * CLIPS * PATCHES * FRAMES * DIM * HEADS * FEAT + 2 * CLIPS * HEADS * PATCHES * FRAMES * FRAMES * FEAT
 
 P = 128
-PASSES = DIM // 512
-CHUNKS = 8
+K_PASS = 512
+BLOCKS = DIM // K_PASS
+TOKENS = 512
+CHUNKS = CLIPS * PATCHES * FRAMES // TOKENS
 SLOTS = HEADS * CHUNKS
+GROUPS = SLOTS // 4
+ROWS = 16
 SCALE = 1.0 / 96.0
+
 W_SLOTS = (0, 2, 4, 6)
 W_SLOTS_FIRST = (1, 3, 4, 6)
-LAST = SLOTS // 4 - 1
+W_LOAD_AHEAD = 2
 
 
 def tile_dividedspacetimeattention_pa_l_kernel(tc, x, Wq, bq, k, out):
@@ -50,30 +55,30 @@ def tile_dividedspacetimeattention_pa_l_kernel(tc, x, Wq, bq, k, out):
         x_codes = []
         x_scales = []
         for c in range(CHUNKS):
-            x_codes.append(keep.tile([P, PASSES, 512], U32, name="x_codes%d" % c, align_bytes=64))
-            x_scales.append(keep.tile([P, PASSES, 512], U8, name="x_scales%d" % c, align_bytes=64))
+            x_codes.append(keep.tile([P, BLOCKS, TOKENS], U32, name="x_codes%d" % c, align_bytes=256))
+            x_scales.append(keep.tile([P, BLOCKS, TOKENS], U8, name="x_scales%d" % c, align_bytes=256))
 
-        xraw, xsrt, xbanks, xgrp = {}, {}, {}, {}
-        kraw, ksrt, kbanks, kgrp, kcodes = {}, {}, {}, {}, {}
-        wraw, wgrp, wcodes = {}, {}, {}
-        qrows, qgrp, qcodes = {}, {}, {}
-        scores, probs = {}, {}
+        x_raw, x_sorted, x_banks, x_grouped = {}, {}, {}, {}
+        k_raw, k_sorted, k_banks, k_grouped, k_quant = {}, {}, {}, {}, {}
+        w_raw, w_grouped, w_quant = {}, {}, {}
+        q_rows, q_grouped, q_quant = {}, {}, {}
+        scores, probs, stats = {}, {}, {}
 
-        def sort_words(raw, tag):
-            srt = stage.tile([P, 1024], F32, tag=tag, bufs=(3 if tag == "ksrt" else 2), name=tag)
+        def sort_words(raw, tag, depth):
+            words = stage.tile([P, 1024], F32, tag=tag, bufs=depth, name=tag)
             nc.vector.tensor_copy(
-                out=srt[:].rearrange("p (a u w) -> p a w u", a=4, u=2),
+                out=words[:].rearrange("p (a u w) -> p a w u", a=4, u=2),
                 in_=raw[:].bitcast(F32).rearrange("p (a w u) -> p a w u", a=4, u=2),
             )
-            return srt
+            return words
 
-        def turn(srt, order):
+        def transpose_unit(words, order):
             banks = []
             for half in range(2):
                 bank = psum.tile([P, 4, P], F32, tag="tp", bufs=4, name="tp")
                 for q in range(4):
                     lo = (4 * half + q) * P
-                    nc.tensor.transpose(bank[:, q, :], srt[:, lo : lo + P], order[:])
+                    nc.tensor.transpose(bank[:, q, :], words[:, lo : lo + P], order[:])
                 banks.append(bank)
             return banks
 
@@ -81,64 +86,64 @@ def tile_dividedspacetimeattention_pa_l_kernel(tc, x, Wq, bq, k, out):
             b, m = divmod(c, 4)
             raw = stage.tile([P, DIM], BF16, tag="xraw", bufs=4, name="xraw")
             nc.sync.dma_start(out=raw[:], in_=x[b, 4 * m + i : PATCHES * FRAMES : 16, :])
-            xraw[(c, i)] = raw
+            x_raw[(c, i)] = raw
 
         def sort_x(c, i):
-            xsrt[(c, i)] = sort_words(xraw.pop((c, i)), "xsrt")
+            x_sorted[(c, i)] = sort_words(x_raw.pop((c, i)), "xsrt", 2)
             if c + 1 < CHUNKS:
                 load_x(c + 1, i)
 
-        def turn_x(c, i):
-            xbanks[(c, i)] = turn(xsrt.pop((c, i)), perm)
+        def transpose_x(c, i):
+            x_banks[(c, i)] = transpose_unit(x_sorted.pop((c, i)), perm)
 
-        def out_x(c, i):
-            banks = xbanks.pop((c, i))
-            grp = stage.tile([P, 2048], BF16, tag="xgrp", bufs=3, name="xgrp", align_bytes=64)
-            words = grp[:].bitcast(F32).rearrange("p (g r u) -> p g r u", g=4, u=2)
+        def copy_out_x(c, i):
+            banks = x_banks.pop((c, i))
+            grouped = stage.tile([P, 2048], BF16, tag="xgrp", bufs=3, name="xgrp", align_bytes=64)
+            words = grouped[:].bitcast(F32).rearrange("p (a r u) -> p a r u", a=4, u=2)
             for half in range(2):
                 nc.scalar.copy(
                     out=words[:, 2 * half : 2 * half + 2, :, :],
-                    in_=banks[half][:].rearrange("p (g u) r -> p g r u", u=2),
+                    in_=banks[half][:].rearrange("p (a u) r -> p a r u", u=2),
                 )
-            xgrp[(c, i)] = grp
+            x_grouped[(c, i)] = grouped
 
-        def quant_x(c, i):
-            grp = xgrp.pop((c, i))
-            for g in range(PASSES):
+        def quantize_x(c, i):
+            grouped = x_grouped.pop((c, i))
+            for a in range(BLOCKS):
                 nc.vector.quantize_mx(
-                    out=x_codes[c][:, g, i * P : (i + 1) * P].bitcast(FP8X4),
-                    scales=x_scales[c][:, g, i * P : (i + 1) * P],
-                    in_=grp[:, g * 512 : (g + 1) * 512],
+                    out=x_codes[c][:, a, i * P : (i + 1) * P].bitcast(FP8X4),
+                    scales=x_scales[c][:, a, i * P : (i + 1) * P],
+                    in_=grouped[:, a * 512 : (a + 1) * 512],
                 )
 
-        def load_w(h, g):
-            raw = stage.tile([P, 4, 512], BF16, tag="wraw", bufs=4, name="wraw")
+        def load_w(h, a):
+            raw = stage.tile([P, 4, FEAT], BF16, tag="wraw", bufs=4, name="wraw")
             nc.sync.dma_start(
                 out=raw[:],
-                in_=Wq[512 * g : 512 * (g + 1), 512 * h : 512 * (h + 1)].rearrange("(p j) c -> p j c", j=4),
+                in_=Wq[K_PASS * a : K_PASS * (a + 1), FEAT * h : FEAT * (h + 1)].rearrange("(p r) c -> p r c", r=4),
             )
-            wraw[(h, g)] = raw
+            w_raw[(h, a)] = raw
 
-        def group_w(h, g, shared):
-            raw = wraw.pop((h, g))
-            grp = stage.tile([P, 2048], BF16, tag="wgrp", bufs=2, name="wgrp", align_bytes=64)
-            dst = grp[:].rearrange("p (t m j) -> p m t j", t=4, j=4)
-            src = raw[:].rearrange("p j (m t) -> p m t j", t=4)
-            if shared:
+        def group_w(h, a, with_scalar):
+            raw = w_raw.pop((h, a))
+            grouped = stage.tile([P, 2048], BF16, tag="wgrp", bufs=2, name="wgrp", align_bytes=64)
+            dst = grouped[:].rearrange("p (t w r) -> p w t r", t=4, r=4)
+            src = raw[:].rearrange("p r (w t) -> p w t r", t=4)
+            if with_scalar:
                 nc.vector.tensor_copy(out=dst[:, :, 0:2, :], in_=src[:, :, 0:2, :])
                 nc.scalar.copy(out=dst[:, :, 2:4, :], in_=src[:, :, 2:4, :])
             else:
                 nc.vector.tensor_copy(out=dst, in_=src)
-            wgrp[(h, g)] = grp
+            w_grouped[(h, a)] = grouped
 
-        def quant_w(h, g):
-            grp = wgrp.pop((h, g))
-            if g == 0:
-                wc = stage.tile([P, PASSES, 512], U32, tag="wc", bufs=2, name="wc", align_bytes=64)
-                ws = stage.tile([P, PASSES, 512], U8, tag="ws", bufs=2, name="ws", align_bytes=64)
-                wcodes[h] = (wc, ws)
-            wc, ws = wcodes[h]
-            nc.vector.quantize_mx(out=wc[:, g, :].bitcast(FP8X4), scales=ws[:, g, :], in_=grp[:])
+        def quantize_w(h, a):
+            grouped = w_grouped.pop((h, a))
+            if a == 0:
+                codes = stage.tile([P, BLOCKS, FEAT], U32, tag="wc", bufs=2, name="wc", align_bytes=256)
+                scales = stage.tile([P, BLOCKS, FEAT], U8, tag="ws", bufs=2, name="ws", align_bytes=256)
+                w_quant[h] = (codes, scales)
+            codes, scales = w_quant[h]
+            nc.vector.quantize_mx(out=codes[:, a, :].bitcast(FP8X4), scales=scales[:, a, :], in_=grouped[:])
 
         def load_k(s):
             h, c = divmod(s, CHUNKS)
@@ -148,52 +153,52 @@ def tile_dividedspacetimeattention_pa_l_kernel(tc, x, Wq, bq, k, out):
                 out=raw[:].rearrange("p (j d) -> p j d", j=4),
                 in_=k[b, h].rearrange("(j q) g d -> (q g) j d", j=4)[P * m : P * (m + 1), :, :],
             )
-            kraw[s] = raw
+            k_raw[s] = raw
 
         def sort_k(s):
-            ksrt[s] = sort_words(kraw.pop(s), "ksrt")
+            k_sorted[s] = sort_words(k_raw.pop(s), "ksrt", 3)
 
-        def turn_k(s):
-            kbanks[s] = turn(ksrt.pop(s), ident)
+        def transpose_k(s):
+            k_banks[s] = transpose_unit(k_sorted.pop(s), ident)
 
-        def out_k(s, half):
+        def copy_out_k(s, half):
             if half == 0:
-                kgrp[s] = stage.tile([P, 2048], BF16, tag="kgrp", bufs=2, name="kgrp", align_bytes=64)
-            words = kgrp[s][:].bitcast(F32).rearrange("p (i j g u) -> p i j g u", i=4, j=4, u=2)
-            bank = kbanks[s][half]
+                k_grouped[s] = stage.tile([P, 2048], BF16, tag="kgrp", bufs=2, name="kgrp", align_bytes=64)
+            words = k_grouped[s][:].bitcast(F32).rearrange("p (i j g u) -> p i j g u", i=4, j=4, u=2)
+            bank = k_banks[s][half]
             for q in range(2):
                 nc.scalar.copy(
                     out=words[:, :, 2 * half + q, :, :],
                     in_=bank[:, 2 * q : 2 * q + 2, :].rearrange("p u (i g) -> p i g u", i=4),
                 )
             if half == 1:
-                kbanks.pop(s)
+                k_banks.pop(s)
 
-        def quant_k(s):
-            grp = kgrp.pop(s)
-            kc = stage.tile([P, 512], U32, tag="kc", bufs=3, name="kc", align_bytes=64)
-            ks = stage.tile([P, 512], U8, tag="ks", bufs=3, name="ks", align_bytes=64)
-            nc.vector.quantize_mx(out=kc[:].bitcast(FP8X4), scales=ks[:], in_=grp[:])
-            kcodes[s] = (kc, ks)
+        def quantize_k(s):
+            grouped = k_grouped.pop(s)
+            codes = stage.tile([P, TOKENS], U32, tag="kc", bufs=3, name="kc", align_bytes=256)
+            scales = stage.tile([P, TOKENS], U8, tag="ks", bufs=3, name="ks", align_bytes=256)
+            nc.vector.quantize_mx(out=codes[:].bitcast(FP8X4), scales=scales[:], in_=grouped[:])
+            k_quant[s] = (codes, scales)
 
         def project(s, t):
             h, c = divmod(s, CHUNKS)
-            wc, ws = wcodes[h]
-            acc = psum.tile([P, 512], F32, tag="acc", bufs=3, name="acc")
-            for g in range(PASSES):
+            codes, scales = w_quant[h]
+            acc = psum.tile([P, TOKENS], F32, tag="acc", bufs=3, name="acc")
+            for a in range(BLOCKS):
                 nc.tensor.matmul_mx(
                     out=acc[:],
-                    lhsT=wc[:, g, t * P : (t + 1) * P].bitcast(FP8X4),
-                    lhsT_scale=ws[:, g, t * P : (t + 1) * P],
-                    rhs=x_codes[c][:, g, :].bitcast(FP8X4),
-                    rhs_scale=x_scales[c][:, g, :],
-                    start=(g == 0),
-                    stop=(g == PASSES - 1),
+                    lhsT=codes[:, a, t * P : (t + 1) * P].bitcast(FP8X4),
+                    lhsT_scale=scales[:, a, t * P : (t + 1) * P],
+                    rhs=x_codes[c][:, a, :].bitcast(FP8X4),
+                    rhs_scale=x_scales[c][:, a, :],
+                    start=(a == 0),
+                    stop=(a == BLOCKS - 1),
                 )
             if t == 0:
-                qrows[s] = stage.tile([P, 4, 512], BF16, tag="qb", bufs=2, name="qb")
+                q_rows[s] = stage.tile([P, 4, TOKENS], BF16, tag="qb", bufs=2, name="qb")
             nc.scalar.activation(
-                out=qrows[s][:, t, :],
+                out=q_rows[s][:, t, :],
                 in_=acc[:],
                 func=ACT.Identity,
                 bias=bias[:, 4 * h + t : 4 * h + t + 1],
@@ -201,93 +206,88 @@ def tile_dividedspacetimeattention_pa_l_kernel(tc, x, Wq, bq, k, out):
             )
 
         def group_q(s):
-            rows = qrows.pop(s)
-            grp = stage.tile([P, 2048], BF16, tag="qg", bufs=2, name="qg", align_bytes=64)
+            rows = q_rows.pop(s)
+            grouped = stage.tile([P, 2048], BF16, tag="qg", bufs=2, name="qg", align_bytes=64)
             nc.vector.tensor_copy(
-                out=grp[:].rearrange("p (c i t) -> p c t i", i=4, t=4),
-                in_=rows[:].rearrange("p t (c i) -> p c t i", i=4),
+                out=grouped[:].rearrange("p (c v t) -> p c t v", v=4, t=4),
+                in_=rows[:].rearrange("p t (c v) -> p c t v", v=4),
             )
-            qgrp[s] = grp
+            q_grouped[s] = grouped
 
-        def quant_q(s):
-            grp = qgrp.pop(s)
-            qc = stage.tile([P, 512], U32, tag="qc", bufs=2, name="qc", align_bytes=64)
-            qs = stage.tile([P, 512], U8, tag="qs", bufs=2, name="qs", align_bytes=64)
-            nc.vector.quantize_mx(out=qc[:].bitcast(FP8X4), scales=qs[:], in_=grp[:])
-            qcodes[s] = (qc, qs)
+        def quantize_q(s):
+            grouped = q_grouped.pop(s)
+            codes = stage.tile([P, TOKENS], U32, tag="qc", bufs=2, name="qc", align_bytes=256)
+            scales = stage.tile([P, TOKENS], U8, tag="qs", bufs=2, name="qs", align_bytes=256)
+            nc.vector.quantize_mx(out=codes[:].bitcast(FP8X4), scales=scales[:], in_=grouped[:])
+            q_quant[s] = (codes, scales)
 
         def score(s):
-            qc, qs = qcodes.pop(s)
-            kc, ks = kcodes.pop(s)
-            sc = psum.tile([P, 4, P], F32, tag="sc", bufs=1, name="sc")
+            q_codes, q_scales = q_quant.pop(s)
+            k_codes, k_scales = k_quant.pop(s)
+            bank = psum.tile([P, 4, P], F32, tag="sc", bufs=1, name="sc")
             for i in range(4):
                 nc.tensor.matmul_mx(
-                    out=sc[:, i, :],
-                    lhsT=qc[:, i * P : (i + 1) * P].bitcast(FP8X4),
-                    lhsT_scale=qs[:, i * P : (i + 1) * P],
-                    rhs=kc[:, i * P : (i + 1) * P].bitcast(FP8X4),
-                    rhs_scale=ks[:, i * P : (i + 1) * P],
+                    out=bank[:, i, :],
+                    lhsT=q_codes[:, i * P : (i + 1) * P].bitcast(FP8X4),
+                    lhsT_scale=q_scales[:, i * P : (i + 1) * P],
+                    rhs=k_codes[:, i * P : (i + 1) * P].bitcast(FP8X4),
+                    rhs_scale=k_scales[:, i * P : (i + 1) * P],
                     start=True,
                     stop=True,
                 )
-            return sc
-
-        def pick(s, sc):
-            grp, m = divmod(s, 4)
+            group, m = divmod(s, 4)
             if m == 0:
-                scores[grp] = stage.tile([P, 16, FRAMES], F32, tag="cmp", bufs=2, name="cmp")
+                scores[group] = stage.tile([P, ROWS, FRAMES], F32, tag="cmp", bufs=2, name="cmp")
             for j in range(4):
                 lo = 32 * j
                 nc.scalar.copy(
-                    out=scores[grp][lo : lo + 32, 4 * m : 4 * m + 4, :],
-                    in_=sc[lo : lo + 32, :, lo : lo + 32],
+                    out=scores[group][lo : lo + 32, 4 * m : 4 * m + 4, :],
+                    in_=bank[lo : lo + 32, :, lo : lo + 32],
                 )
 
-        stats = {}
+        def soft_max(group, lo, hi):
+            top = stage.tile([P, ROWS], F32, tag="mx", bufs=2, name="mx")
+            nc.vector.tensor_reduce(out=top[:, lo:hi], in_=scores[group][:, lo:hi, :], axis=AXIS.X, op=ALU.max)
+            stats[(group, lo)] = top
 
-        def soft_max(grp, lo, hi):
-            mx = stage.tile([P, 16], F32, tag="mx", bufs=2, name="mx")
-            nc.vector.tensor_reduce(out=mx[:, lo:hi], in_=scores[grp][:, lo:hi, :], axis=AXIS.X, op=ALU.max)
-            stats[(grp, lo)] = mx
-
-        def soft_sub(grp, lo, hi):
-            mx = stats.pop((grp, lo))
+        def soft_sub(group, lo, hi):
+            top = stats.pop((group, lo))
             nc.vector.tensor_tensor(
-                out=scores[grp][:, lo:hi, :],
-                in0=scores[grp][:, lo:hi, :],
-                in1=mx[:, lo:hi].unsqueeze(2).to_broadcast([P, hi - lo, FRAMES]),
+                out=scores[group][:, lo:hi, :],
+                in0=scores[group][:, lo:hi, :],
+                in1=top[:, lo:hi].unsqueeze(2).to_broadcast([P, hi - lo, FRAMES]),
                 op=ALU.subtract,
             )
 
-        def soft_exp(grp, lo, hi):
+        def soft_exp(group, lo, hi):
             if lo == 0:
-                probs[grp] = stage.tile([P, 16, FRAMES], F32, tag="ex", bufs=2, name="ex")
-            nc.scalar.activation(out=probs[grp][:, lo:hi, :], in_=scores[grp][:, lo:hi, :], func=ACT.Exp, scale=SCALE)
+                probs[group] = stage.tile([P, ROWS, FRAMES], F32, tag="ex", bufs=2, name="ex")
+            nc.scalar.activation(out=probs[group][:, lo:hi, :], in_=scores[group][:, lo:hi, :], func=ACT.Exp, scale=SCALE)
 
-        def soft_sum(grp, lo, hi):
-            sm = stage.tile([P, 16], F32, tag="sm", bufs=2, name="sm")
-            nc.vector.tensor_reduce(out=sm[:, lo:hi], in_=probs[grp][:, lo:hi, :], axis=AXIS.X, op=ALU.add)
-            stats[(grp, lo)] = sm
+        def soft_sum(group, lo, hi):
+            total = stage.tile([P, ROWS], F32, tag="sm", bufs=2, name="sm")
+            nc.vector.tensor_reduce(out=total[:, lo:hi], in_=probs[group][:, lo:hi, :], axis=AXIS.X, op=ALU.add)
+            stats[(group, lo)] = total
 
-        def soft_recip(grp, lo, hi):
-            rs = stage.tile([P, 16], F32, tag="rs", bufs=2, name="rs")
-            nc.vector.reciprocal(out=rs[:, lo:hi], in_=stats.pop((grp, lo))[:, lo:hi])
-            stats[(grp, lo)] = rs
+        def soft_recip(group, lo, hi):
+            inverse = stage.tile([P, ROWS], F32, tag="rs", bufs=2, name="rs")
+            nc.vector.reciprocal(out=inverse[:, lo:hi], in_=stats.pop((group, lo))[:, lo:hi])
+            stats[(group, lo)] = inverse
 
-        def soft_mul(grp, lo, hi):
-            rs = stats.pop((grp, lo))
+        def soft_mul(group, lo, hi):
+            inverse = stats.pop((group, lo))
             nc.vector.tensor_tensor(
-                out=probs[grp][:, lo:hi, :],
-                in0=probs[grp][:, lo:hi, :],
-                in1=rs[:, lo:hi].unsqueeze(2).to_broadcast([P, hi - lo, FRAMES]),
+                out=probs[group][:, lo:hi, :],
+                in0=probs[group][:, lo:hi, :],
+                in1=inverse[:, lo:hi].unsqueeze(2).to_broadcast([P, hi - lo, FRAMES]),
                 op=ALU.mult,
             )
 
-        def store(grp, lo, hi):
-            h, b = divmod(grp, CLIPS)
+        def store(group, lo, hi):
+            h, b = divmod(group, CLIPS)
             view = out[b, h].rearrange("(j q) f g -> j f q g", j=4)
             for j in range(4):
-                nc.sync.dma_start(out=view[j][:, lo:hi, :], in_=probs[grp][32 * j : 32 * j + 32, lo:hi, :])
+                nc.sync.dma_start(out=view[j][:, lo:hi, :], in_=probs[group][32 * j : 32 * j + 32, lo:hi, :])
 
         k_sort_slot = []
         for s in range(SLOTS):
@@ -300,6 +300,25 @@ def tile_dividedspacetimeattention_pa_l_kernel(tc, x, Wq, bq, k, out):
             else:
                 k_sort_slot.append(s - 3)
         k_load_slot = [(1 if s == 4 else k_sort_slot[s] - 2) for s in range(SLOTS)]
+
+        def w_slot(h, a):
+            return CHUNKS * (h - 1) + (W_SLOTS_FIRST if h == 1 else W_SLOTS)[a]
+
+        def loads_of_slot(s):
+            for unit in range(SLOTS):
+                if k_load_slot[unit] == s:
+                    load_k(unit)
+            for h in range(1, HEADS):
+                for a in range(BLOCKS):
+                    if w_slot(h, a) == s + W_LOAD_AHEAD:
+                        load_w(h, a)
+
+        def w_block_of_slot(s):
+            for h in range(1, HEADS):
+                for a in range(BLOCKS):
+                    if w_slot(h, a) == s:
+                        return (h, a)
+            return None
 
         nc.vector.memset(warm_in[:], 0.0)
         nc.scalar.activation(out=warm_out[:], in_=warm_in[:], func=ACT.Exp)
@@ -314,157 +333,159 @@ def tile_dividedspacetimeattention_pa_l_kernel(tc, x, Wq, bq, k, out):
         nc.sync.dma_start(out=bias_bf[:], in_=bq.rearrange("(h p t) -> p h t", h=HEADS, t=4))
 
         sort_x(0, 0)
-        turn_x(0, 0)
+        transpose_x(0, 0)
         sort_x(0, 1)
-        out_x(0, 0)
-        turn_x(0, 1)
+        copy_out_x(0, 0)
+        transpose_x(0, 1)
         group_w(0, 0, True)
-        quant_x(0, 0)
+        quantize_x(0, 0)
         sort_x(0, 2)
-        out_x(0, 1)
-        turn_x(0, 2)
-        quant_w(0, 0)
+        copy_out_x(0, 1)
+        transpose_x(0, 2)
+        quantize_w(0, 0)
         group_w(0, 1, True)
-        quant_x(0, 1)
+        quantize_x(0, 1)
         sort_x(0, 3)
-        for s in range(SLOTS):
-            if k_load_slot[s] < 0:
-                load_k(s)
-        for g in range(PASSES):
-            if W_SLOTS_FIRST[g] < 2:
-                load_w(1, g)
-        out_x(0, 2)
-        turn_x(0, 3)
-        quant_w(0, 1)
+        for early in (-2, -1):
+            loads_of_slot(early)
+        copy_out_x(0, 2)
+        transpose_x(0, 3)
+        quantize_w(0, 1)
         group_w(0, 2, True)
-        quant_x(0, 2)
-        out_x(0, 3)
-        quant_w(0, 2)
+        quantize_x(0, 2)
+        copy_out_x(0, 3)
+        quantize_w(0, 2)
         group_w(0, 3, True)
-        quant_x(0, 3)
-        quant_w(0, 3)
+        quantize_x(0, 3)
+        quantize_w(0, 3)
         nc.vector.tensor_copy(out=bias[:], in_=bias_bf[:].rearrange("p h t -> p (h t)"))
         sort_x(1, 0)
         sort_x(1, 1)
 
-        for it in range(SLOTS + 1):
-            h, c = divmod(it, CHUNKS)
-            live = it < SLOTS
-            first = it < CHUNKS
-            fresh = it + 1 if it + 1 < CHUNKS else None
-            w_slots = W_SLOTS_FIRST if h == 0 else W_SLOTS
+        for s in range(CHUNKS):
+            loads_of_slot(s)
+            k_units = [0, 1] if s == 1 else ([s] if s >= 2 else [])
+            fresh = s + 1 if s + 1 < CHUNKS else None
+            w_block = w_block_of_slot(s)
 
-            for s in range(SLOTS):
-                if k_load_slot[s] == it:
-                    load_k(s)
-            for hh in (h, h + 1):
-                for g in range(PASSES):
-                    if hh < HEADS - 1 and CHUNKS * hh + (W_SLOTS_FIRST if hh == 0 else W_SLOTS)[g] == it + 2:
-                        load_w(hh + 1, g)
-            if it % 4 == 0 and it >= 8:
-                store((it - 8) // 4, 0, 16)
+            for unit in k_units:
+                copy_out_k(unit, 0)
+                copy_out_k(unit, 1)
+            if s >= 1:
+                group_q(s - 1)
+            for unit in k_units:
+                quantize_k(unit)
+            if s >= 1:
+                quantize_q(s - 1)
+            if s == 5:
+                soft_max(0, 0, ROWS)
+                soft_sub(0, 0, ROWS)
+            if s == 7:
+                soft_sum(0, 0, ROWS)
+                soft_recip(0, 0, ROWS)
+                soft_mul(0, 0, ROWS)
 
-            part_a = (it - 5) // 4 if (it % 4 == 1 and 5 <= it < SLOTS) else None
-            part_b = (it - 7) // 4 if (it % 4 == 3 and 7 <= it < SLOTS) else None
-            w_now = (h + 1, w_slots.index(c)) if (live and h + 1 < HEADS and c in w_slots) else None
-            sorts = [s for s in range(3, SLOTS) if k_sort_slot[s] == it]
-            ks_now = [0, 1] if it == 1 else ([it] if 2 <= it < SLOTS else [])
+            for t in range(4):
+                project(s, t)
+                if fresh is not None:
+                    transpose_x(fresh, t)
+                    copy_out_x(fresh, t)
+                    if t < 2:
+                        sort_x(fresh, t + 2)
+                    if t > 0:
+                        quantize_x(fresh, t - 1)
+                if t == 0 and w_block is not None:
+                    group_w(w_block[0], w_block[1], False)
+                if t == 3 and s == 5:
+                    soft_exp(0, 0, ROWS)
 
-            if first:
-                for s in ks_now:
-                    out_k(s, 0)
-                    out_k(s, 1)
-            if 1 <= it:
-                group_q(it - 1)
-            if first:
-                for s in ks_now:
-                    quant_k(s)
-            elif part_a is not None:
-                soft_max(part_a, 0, 16)
-            elif part_b is not None:
-                soft_sum(part_b, 0, 16)
-            elif it == SLOTS:
-                soft_max(LAST, 0, 12)
-            else:
-                for s in sorts:
-                    sort_k(s)
-                sorts = []
-            if 1 <= it:
-                quant_q(it - 1)
-            if first and part_a is not None:
-                soft_max(part_a, 0, 16)
-            if first and part_b is not None:
-                soft_sum(part_b, 0, 16)
-            if part_b is not None:
-                soft_recip(part_b, 0, 16)
-            if not first:
-                for s in sorts:
-                    sort_k(s)
-                sorts = []
-            if part_a is not None:
-                soft_sub(part_a, 0, 16)
-            if part_b is not None:
-                soft_mul(part_b, 0, 16)
-            if it == SLOTS:
-                soft_sub(LAST, 0, 12)
-                soft_exp(LAST, 0, 12)
-            if w_now is not None and not first:
-                group_w(w_now[0], w_now[1], False)
+            for unit in range(SLOTS):
+                if k_sort_slot[unit] == s and unit != 2:
+                    sort_k(unit)
+            if w_block is not None:
+                quantize_w(w_block[0], w_block[1])
 
-            if live:
-                for t in range(4):
-                    project(it, t)
-                    if fresh is not None:
-                        turn_x(fresh, t)
-                        out_x(fresh, t)
-                        if t < 2:
-                            sort_x(fresh, t + 2)
-                        if t > 0:
-                            quant_x(fresh, t - 1)
-                    if t == 0 and w_now is not None and first:
-                        group_w(w_now[0], w_now[1], False)
-                    if t < 2 and not first:
-                        out_k(it, t)
-                    if t == 3 and part_a is not None:
-                        soft_exp(part_a, 0, 16)
-
-            if not first and live:
-                quant_k(it)
-            if it == 0:
-                sort_k(0)
-                sort_k(1)
-            for s in sorts:
-                sort_k(s)
-            if w_now is not None:
-                quant_w(w_now[0], w_now[1])
-
-            if 1 <= it:
-                pick(it - 1, score(it - 1))
-            if it == 0:
-                turn_k(0)
-                turn_k(1)
+            if s >= 1:
+                score(s - 1)
+            if s == 0:
+                transpose_k(0)
+                transpose_k(1)
                 sort_k(2)
-            elif it < CHUNKS - 1:
-                turn_k(it + 1)
-            elif it % 2 == 1:
-                for s in (it + 1, it + 2):
-                    if s < SLOTS:
-                        turn_k(s)
+            elif s < CHUNKS - 1:
+                transpose_k(s + 1)
+            else:
+                transpose_k(s + 1)
+                transpose_k(s + 2)
 
             if fresh is not None:
-                quant_x(fresh, 3)
+                quantize_x(fresh, 3)
                 if fresh + 1 < CHUNKS:
                     sort_x(fresh + 1, 0)
                     sort_x(fresh + 1, 1)
 
-        soft_sum(LAST, 0, 12)
-        soft_max(LAST, 12, 16)
-        soft_recip(LAST, 0, 12)
-        soft_sub(LAST, 12, 16)
-        soft_mul(LAST, 0, 12)
-        soft_exp(LAST, 12, 16)
-        store(LAST, 0, 12)
-        soft_sum(LAST, 12, 16)
-        soft_recip(LAST, 12, 16)
-        soft_mul(LAST, 12, 16)
-        store(LAST, 12, 16)
+        for s in range(CHUNKS, SLOTS):
+            loads_of_slot(s)
+            if s % 4 == 0:
+                store((s - 8) // 4, 0, ROWS)
+            first_half = (s - 5) // 4 if s % 4 == 1 else None
+            second_half = (s - 7) // 4 if s % 4 == 3 else None
+            w_block = w_block_of_slot(s)
+            to_sort = [unit for unit in range(SLOTS) if k_sort_slot[unit] == s]
+
+            group_q(s - 1)
+            if first_half is not None:
+                soft_max(first_half, 0, ROWS)
+            elif second_half is not None:
+                soft_sum(second_half, 0, ROWS)
+            else:
+                for unit in to_sort:
+                    sort_k(unit)
+            quantize_q(s - 1)
+            if second_half is not None:
+                soft_recip(second_half, 0, ROWS)
+            if s % 2 == 1:
+                for unit in to_sort:
+                    sort_k(unit)
+            if first_half is not None:
+                soft_sub(first_half, 0, ROWS)
+            if second_half is not None:
+                soft_mul(second_half, 0, ROWS)
+            if w_block is not None:
+                group_w(w_block[0], w_block[1], False)
+
+            for t in range(4):
+                project(s, t)
+                if t < 2:
+                    copy_out_k(s, t)
+                if t == 3 and first_half is not None:
+                    soft_exp(first_half, 0, ROWS)
+
+            quantize_k(s)
+            if w_block is not None:
+                quantize_w(w_block[0], w_block[1])
+            score(s - 1)
+            if s % 2 == 1:
+                for unit in (s + 1, s + 2):
+                    if unit < SLOTS:
+                        transpose_k(unit)
+
+        last = GROUPS - 1
+        split = ROWS - 4
+        store(last - 1, 0, ROWS)
+        group_q(SLOTS - 1)
+        soft_max(last, 0, split)
+        quantize_q(SLOTS - 1)
+        soft_sub(last, 0, split)
+        soft_exp(last, 0, split)
+        score(SLOTS - 1)
+        soft_sum(last, 0, split)
+        soft_max(last, split, ROWS)
+        soft_recip(last, 0, split)
+        soft_sub(last, split, ROWS)
+        soft_mul(last, 0, split)
+        soft_exp(last, split, ROWS)
+        store(last, 0, split)
+        soft_sum(last, split, ROWS)
+        soft_recip(last, split, ROWS)
+        soft_mul(last, split, ROWS)
+        store(last, split, ROWS)

from contextlib import ExitStack

import concourse.mybir as mybir
from concourse.masks import make_identity

F32 = mybir.dt.float32
BF16 = mybir.dt.bfloat16
U32 = mybir.dt.uint32
U8 = mybir.dt.uint8
FP8X4 = mybir.dt.float8_e4m3fn_x4
ACT = mybir.ActivationFunctionType
ALU = mybir.AluOpType
AXIS = mybir.AxisListType

CLIPS, PATCHES, FRAMES, DIM, HEADS, FEAT = 2, 64, 32, 2048, 12, 512
FLOPS = 2 * CLIPS * PATCHES * FRAMES * DIM * HEADS * FEAT + 2 * CLIPS * HEADS * PATCHES * FRAMES * FRAMES * FEAT

P = 128
K_PASS = 512
BLOCKS = DIM // K_PASS
TOKENS = 512
CHUNKS = CLIPS * PATCHES * FRAMES // TOKENS
SLOTS = HEADS * CHUNKS
GROUPS = SLOTS // 4
ROWS = 16
SCALE = 1.0 / 96.0

W_SLOTS = (0, 2, 4, 6)
W_SLOTS_FIRST = (1, 3, 4, 6)
W_LOAD_AHEAD = 2


def tile_dividedspacetimeattention_pa_l_kernel(tc, x, Wq, bq, k, out):
    nc = tc.nc
    with ExitStack() as ctx:
        keep = ctx.enter_context(tc.tile_pool(name="keep", bufs=1))
        stage = ctx.enter_context(tc.tile_pool(name="stage", bufs=2))
        psum = ctx.enter_context(tc.psum_pool(name="psum", bufs=1))

        ident = keep.tile([P, P], F32, name="ident")
        make_identity(nc, ident[:])

        ctx.enter_context(tc.manual_schedule())

        perm = keep.tile([P, P], F32, name="perm")
        nc.vector.tensor_copy(
            out=perm[:].rearrange("p (j f) -> p j f", j=4),
            in_=ident[:].rearrange("p (f j) -> p j f", j=4),
        )

        bias_bf = keep.tile([P, HEADS, 4], BF16, name="bias_bf")
        bias = keep.tile([P, HEADS * 4], F32, name="bias")
        warm_in = keep.tile([P, 1], F32, name="warm_in")
        warm_out = keep.tile([P, 1], F32, name="warm_out")
        x_codes = []
        x_scales = []
        for c in range(CHUNKS):
            x_codes.append(keep.tile([P, BLOCKS, TOKENS], U32, name="x_codes%d" % c, align_bytes=256))
            x_scales.append(keep.tile([P, BLOCKS, TOKENS], U8, name="x_scales%d" % c, align_bytes=256))

        x_raw, x_sorted, x_banks, x_grouped = {}, {}, {}, {}
        k_raw, k_sorted, k_banks, k_grouped, k_quant = {}, {}, {}, {}, {}
        w_raw, w_grouped, w_quant = {}, {}, {}
        q_rows, q_grouped, q_quant = {}, {}, {}
        scores, probs, stats = {}, {}, {}

        def sort_words(raw, tag, depth):
            words = stage.tile([P, 1024], F32, tag=tag, bufs=depth, name=tag)
            nc.vector.tensor_copy(
                out=words[:].rearrange("p (a u w) -> p a w u", a=4, u=2),
                in_=raw[:].bitcast(F32).rearrange("p (a w u) -> p a w u", a=4, u=2),
            )
            return words

        def transpose_unit(words, order):
            banks = []
            for half in range(2):
                bank = psum.tile([P, 4, P], F32, tag="tp", bufs=4, name="tp")
                for q in range(4):
                    lo = (4 * half + q) * P
                    nc.tensor.transpose(bank[:, q, :], words[:, lo : lo + P], order[:])
                banks.append(bank)
            return banks

        def load_x(c, i):
            b, m = divmod(c, 4)
            raw = stage.tile([P, DIM], BF16, tag="xraw", bufs=4, name="xraw")
            nc.sync.dma_start(out=raw[:], in_=x[b, 4 * m + i : PATCHES * FRAMES : 16, :])
            x_raw[(c, i)] = raw

        def sort_x(c, i):
            x_sorted[(c, i)] = sort_words(x_raw.pop((c, i)), "xsrt", 2)
            if c + 1 < CHUNKS:
                load_x(c + 1, i)

        def transpose_x(c, i):
            x_banks[(c, i)] = transpose_unit(x_sorted.pop((c, i)), perm)

        def copy_out_x(c, i):
            banks = x_banks.pop((c, i))
            grouped = stage.tile([P, 2048], BF16, tag="xgrp", bufs=3, name="xgrp", align_bytes=64)
            words = grouped[:].bitcast(F32).rearrange("p (a r u) -> p a r u", a=4, u=2)
            for half in range(2):
                nc.scalar.copy(
                    out=words[:, 2 * half : 2 * half + 2, :, :],
                    in_=banks[half][:].rearrange("p (a u) r -> p a r u", u=2),
                )
            x_grouped[(c, i)] = grouped

        def quantize_x(c, i):
            grouped = x_grouped.pop((c, i))
            for a in range(BLOCKS):
                nc.vector.quantize_mx(
                    out=x_codes[c][:, a, i * P : (i + 1) * P].bitcast(FP8X4),
                    scales=x_scales[c][:, a, i * P : (i + 1) * P],
                    in_=grouped[:, a * 512 : (a + 1) * 512],
                )

        def load_w(h, a):
            raw = stage.tile([P, 4, FEAT], BF16, tag="wraw", bufs=4, name="wraw")
            nc.sync.dma_start(
                out=raw[:],
                in_=Wq[K_PASS * a : K_PASS * (a + 1), FEAT * h : FEAT * (h + 1)].rearrange("(p r) c -> p r c", r=4),
            )
            w_raw[(h, a)] = raw

        def group_w(h, a, with_scalar):
            raw = w_raw.pop((h, a))
            grouped = stage.tile([P, 2048], BF16, tag="wgrp", bufs=2, name="wgrp", align_bytes=64)
            dst = grouped[:].rearrange("p (t w r) -> p w t r", t=4, r=4)
            src = raw[:].rearrange("p r (w t) -> p w t r", t=4)
            if with_scalar:
                nc.vector.tensor_copy(out=dst[:, :, 0:2, :], in_=src[:, :, 0:2, :])
                nc.scalar.copy(out=dst[:, :, 2:4, :], in_=src[:, :, 2:4, :])
            else:
                nc.vector.tensor_copy(out=dst, in_=src)
            w_grouped[(h, a)] = grouped

        def quantize_w(h, a):
            grouped = w_grouped.pop((h, a))
            if a == 0:
                codes = stage.tile([P, BLOCKS, FEAT], U32, tag="wc", bufs=2, name="wc", align_bytes=256)
                scales = stage.tile([P, BLOCKS, FEAT], U8, tag="ws", bufs=2, name="ws", align_bytes=256)
                w_quant[h] = (codes, scales)
            codes, scales = w_quant[h]
            nc.vector.quantize_mx(out=codes[:, a, :].bitcast(FP8X4), scales=scales[:, a, :], in_=grouped[:])

        def load_k(s):
            h, c = divmod(s, CHUNKS)
            b, m = divmod(c, 4)
            raw = stage.tile([P, 2048], BF16, tag="kraw", bufs=4, name="kraw")
            nc.sync.dma_start(
                out=raw[:].rearrange("p (j d) -> p j d", j=4),
                in_=k[b, h].rearrange("(j q) g d -> (q g) j d", j=4)[P * m : P * (m + 1), :, :],
            )
            k_raw[s] = raw

        def sort_k(s):
            k_sorted[s] = sort_words(k_raw.pop(s), "ksrt", 3)

        def transpose_k(s):
            k_banks[s] = transpose_unit(k_sorted.pop(s), ident)

        def copy_out_k(s, half):
            if half == 0:
                k_grouped[s] = stage.tile([P, 2048], BF16, tag="kgrp", bufs=2, name="kgrp", align_bytes=64)
            words = k_grouped[s][:].bitcast(F32).rearrange("p (i j g u) -> p i j g u", i=4, j=4, u=2)
            bank = k_banks[s][half]
            for q in range(2):
                nc.scalar.copy(
                    out=words[:, :, 2 * half + q, :, :],
                    in_=bank[:, 2 * q : 2 * q + 2, :].rearrange("p u (i g) -> p i g u", i=4),
                )
            if half == 1:
                k_banks.pop(s)

        def quantize_k(s):
            grouped = k_grouped.pop(s)
            codes = stage.tile([P, TOKENS], U32, tag="kc", bufs=3, name="kc", align_bytes=256)
            scales = stage.tile([P, TOKENS], U8, tag="ks", bufs=3, name="ks", align_bytes=256)
            nc.vector.quantize_mx(out=codes[:].bitcast(FP8X4), scales=scales[:], in_=grouped[:])
            k_quant[s] = (codes, scales)

        def project(s, t):
            h, c = divmod(s, CHUNKS)
            codes, scales = w_quant[h]
            acc = psum.tile([P, TOKENS], F32, tag="acc", bufs=3, name="acc")
            for a in range(BLOCKS):
                nc.tensor.matmul_mx(
                    out=acc[:],
                    lhsT=codes[:, a, t * P : (t + 1) * P].bitcast(FP8X4),
                    lhsT_scale=scales[:, a, t * P : (t + 1) * P],
                    rhs=x_codes[c][:, a, :].bitcast(FP8X4),
                    rhs_scale=x_scales[c][:, a, :],
                    start=(a == 0),
                    stop=(a == BLOCKS - 1),
                )
            if t == 0:
                q_rows[s] = stage.tile([P, 4, TOKENS], BF16, tag="qb", bufs=2, name="qb")
            nc.scalar.activation(
                out=q_rows[s][:, t, :],
                in_=acc[:],
                func=ACT.Identity,
                bias=bias[:, 4 * h + t : 4 * h + t + 1],
                scale=1.0,
            )

        def group_q(s):
            rows = q_rows.pop(s)
            grouped = stage.tile([P, 2048], BF16, tag="qg", bufs=2, name="qg", align_bytes=64)
            nc.vector.tensor_copy(
                out=grouped[:].rearrange("p (c v t) -> p c t v", v=4, t=4),
                in_=rows[:].rearrange("p t (c v) -> p c t v", v=4),
            )
            q_grouped[s] = grouped

        def quantize_q(s):
            grouped = q_grouped.pop(s)
            codes = stage.tile([P, TOKENS], U32, tag="qc", bufs=2, name="qc", align_bytes=256)
            scales = stage.tile([P, TOKENS], U8, tag="qs", bufs=2, name="qs", align_bytes=256)
            nc.vector.quantize_mx(out=codes[:].bitcast(FP8X4), scales=scales[:], in_=grouped[:])
            q_quant[s] = (codes, scales)

        def score(s):
            q_codes, q_scales = q_quant.pop(s)
            k_codes, k_scales = k_quant.pop(s)
            bank = psum.tile([P, 4, P], F32, tag="sc", bufs=1, name="sc")
            for i in range(4):
                nc.tensor.matmul_mx(
                    out=bank[:, i, :],
                    lhsT=q_codes[:, i * P : (i + 1) * P].bitcast(FP8X4),
                    lhsT_scale=q_scales[:, i * P : (i + 1) * P],
                    rhs=k_codes[:, i * P : (i + 1) * P].bitcast(FP8X4),
                    rhs_scale=k_scales[:, i * P : (i + 1) * P],
                    start=True,
                    stop=True,
                )
            group, m = divmod(s, 4)
            if m == 0:
                scores[group] = stage.tile([P, ROWS, FRAMES], F32, tag="cmp", bufs=2, name="cmp")
            for j in range(4):
                lo = 32 * j
                nc.scalar.copy(
                    out=scores[group][lo : lo + 32, 4 * m : 4 * m + 4, :],
                    in_=bank[lo : lo + 32, :, lo : lo + 32],
                )

        def soft_max(group, lo, hi):
            top = stage.tile([P, ROWS], F32, tag="mx", bufs=2, name="mx")
            nc.vector.tensor_reduce(out=top[:, lo:hi], in_=scores[group][:, lo:hi, :], axis=AXIS.X, op=ALU.max)
            stats[(group, lo)] = top

        def soft_sub(group, lo, hi):
            top = stats.pop((group, lo))
            nc.vector.tensor_tensor(
                out=scores[group][:, lo:hi, :],
                in0=scores[group][:, lo:hi, :],
                in1=top[:, lo:hi].unsqueeze(2).to_broadcast([P, hi - lo, FRAMES]),
                op=ALU.subtract,
            )

        def soft_exp(group, lo, hi):
            if lo == 0:
                probs[group] = stage.tile([P, ROWS, FRAMES], F32, tag="ex", bufs=2, name="ex")
            nc.scalar.activation(out=probs[group][:, lo:hi, :], in_=scores[group][:, lo:hi, :], func=ACT.Exp, scale=SCALE)

        def soft_sum(group, lo, hi):
            total = stage.tile([P, ROWS], F32, tag="sm", bufs=2, name="sm")
            nc.vector.tensor_reduce(out=total[:, lo:hi], in_=probs[group][:, lo:hi, :], axis=AXIS.X, op=ALU.add)
            stats[(group, lo)] = total

        def soft_recip(group, lo, hi):
            inverse = stage.tile([P, ROWS], F32, tag="rs", bufs=2, name="rs")
            nc.vector.reciprocal(out=inverse[:, lo:hi], in_=stats.pop((group, lo))[:, lo:hi])
            stats[(group, lo)] = inverse

        def soft_mul(group, lo, hi):
            inverse = stats.pop((group, lo))
            nc.vector.tensor_tensor(
                out=probs[group][:, lo:hi, :],
                in0=probs[group][:, lo:hi, :],
                in1=inverse[:, lo:hi].unsqueeze(2).to_broadcast([P, hi - lo, FRAMES]),
                op=ALU.mult,
            )

        def store(group, lo, hi):
            h, b = divmod(group, CLIPS)
            view = out[b, h].rearrange("(j q) f g -> j f q g", j=4)
            for j in range(4):
                nc.sync.dma_start(out=view[j][:, lo:hi, :], in_=probs[group][32 * j : 32 * j + 32, lo:hi, :])

        k_sort_slot = []
        for s in range(SLOTS):
            if s < 3:
                k_sort_slot.append(0)
            elif s <= CHUNKS + 1:
                k_sort_slot.append(s - 2)
            elif s == CHUNKS + 2:
                k_sort_slot.append(CHUNKS - 1)
            else:
                k_sort_slot.append(s - 3)
        k_load_slot = [(1 if s == 4 else k_sort_slot[s] - 2) for s in range(SLOTS)]

        def w_slot(h, a):
            return CHUNKS * (h - 1) + (W_SLOTS_FIRST if h == 1 else W_SLOTS)[a]

        def loads_of_slot(s):
            for unit in range(SLOTS):
                if k_load_slot[unit] == s:
                    load_k(unit)
            for h in range(1, HEADS):
                for a in range(BLOCKS):
                    if w_slot(h, a) == s + W_LOAD_AHEAD:
                        load_w(h, a)

        def w_block_of_slot(s):
            for h in range(1, HEADS):
                for a in range(BLOCKS):
                    if w_slot(h, a) == s:
                        return (h, a)
            return None

        nc.vector.memset(warm_in[:], 0.0)
        nc.scalar.activation(out=warm_out[:], in_=warm_in[:], func=ACT.Exp)
        load_x(0, 0)
        load_x(0, 1)
        load_w(0, 0)
        load_x(0, 2)
        load_w(0, 1)
        load_x(0, 3)
        load_w(0, 2)
        load_w(0, 3)
        nc.sync.dma_start(out=bias_bf[:], in_=bq.rearrange("(h p t) -> p h t", h=HEADS, t=4))

        sort_x(0, 0)
        transpose_x(0, 0)
        sort_x(0, 1)
        copy_out_x(0, 0)
        transpose_x(0, 1)
        group_w(0, 0, True)
        quantize_x(0, 0)
        sort_x(0, 2)
        copy_out_x(0, 1)
        transpose_x(0, 2)
        quantize_w(0, 0)
        group_w(0, 1, True)
        quantize_x(0, 1)
        sort_x(0, 3)
        for early in (-2, -1):
            loads_of_slot(early)
        copy_out_x(0, 2)
        transpose_x(0, 3)
        quantize_w(0, 1)
        group_w(0, 2, True)
        quantize_x(0, 2)
        copy_out_x(0, 3)
        quantize_w(0, 2)
        group_w(0, 3, True)
        quantize_x(0, 3)
        quantize_w(0, 3)
        nc.vector.tensor_copy(out=bias[:], in_=bias_bf[:].rearrange("p h t -> p (h t)"))
        sort_x(1, 0)
        sort_x(1, 1)

        for s in range(CHUNKS):
            loads_of_slot(s)
            k_units = [0, 1] if s == 1 else ([s] if s >= 2 else [])
            fresh = s + 1 if s + 1 < CHUNKS else None
            w_block = w_block_of_slot(s)

            for unit in k_units:
                copy_out_k(unit, 0)
                copy_out_k(unit, 1)
            if s >= 1:
                group_q(s - 1)
            for unit in k_units:
                quantize_k(unit)
            if s >= 1:
                quantize_q(s - 1)
            if s == 5:
                soft_max(0, 0, ROWS)
                soft_sub(0, 0, ROWS)
            if s == 7:
                soft_sum(0, 0, ROWS)
                soft_recip(0, 0, ROWS)
                soft_mul(0, 0, ROWS)

            for t in range(4):
                project(s, t)
                if fresh is not None:
                    transpose_x(fresh, t)
                    copy_out_x(fresh, t)
                    if t < 2:
                        sort_x(fresh, t + 2)
                    if t > 0:
                        quantize_x(fresh, t - 1)
                if t == 0 and w_block is not None:
                    group_w(w_block[0], w_block[1], False)
                if t == 3 and s == 5:
                    soft_exp(0, 0, ROWS)

            for unit in range(SLOTS):
                if k_sort_slot[unit] == s and unit != 2:
                    sort_k(unit)
            if w_block is not None:
                quantize_w(w_block[0], w_block[1])

            if s >= 1:
                score(s - 1)
            if s == 0:
                transpose_k(0)
                transpose_k(1)
                sort_k(2)
            elif s < CHUNKS - 1:
                transpose_k(s + 1)
            else:
                transpose_k(s + 1)
                transpose_k(s + 2)

            if fresh is not None:
                quantize_x(fresh, 3)
                if fresh + 1 < CHUNKS:
                    sort_x(fresh + 1, 0)
                    sort_x(fresh + 1, 1)

        for s in range(CHUNKS, SLOTS):
            loads_of_slot(s)
            if s % 4 == 0:
                store((s - 8) // 4, 0, ROWS)
            first_half = (s - 5) // 4 if s % 4 == 1 else None
            second_half = (s - 7) // 4 if s % 4 == 3 else None
            w_block = w_block_of_slot(s)
            to_sort = [unit for unit in range(SLOTS) if k_sort_slot[unit] == s]

            group_q(s - 1)
            if first_half is not None:
                soft_max(first_half, 0, ROWS)
            elif second_half is not None:
                soft_sum(second_half, 0, ROWS)
            else:
                for unit in to_sort:
                    sort_k(unit)
            quantize_q(s - 1)
            if second_half is not None:
                soft_recip(second_half, 0, ROWS)
            if s % 2 == 1:
                for unit in to_sort:
                    sort_k(unit)
            if first_half is not None:
                soft_sub(first_half, 0, ROWS)
            if second_half is not None:
                soft_mul(second_half, 0, ROWS)
            if w_block is not None:
                group_w(w_block[0], w_block[1], False)

            for t in range(4):
                project(s, t)
                if t < 2:
                    copy_out_k(s, t)
                if t == 3 and first_half is not None:
                    soft_exp(first_half, 0, ROWS)

            quantize_k(s)
            if w_block is not None:
                quantize_w(w_block[0], w_block[1])
            score(s - 1)
            if s % 2 == 1:
                for unit in (s + 1, s + 2):
                    if unit < SLOTS:
                        transpose_k(unit)

        last = GROUPS - 1
        split = ROWS - 4
        store(last - 1, 0, ROWS)
        group_q(SLOTS - 1)
        soft_max(last, 0, split)
        quantize_q(SLOTS - 1)
        soft_sub(last, 0, split)
        soft_exp(last, 0, split)
        score(SLOTS - 1)
        soft_sum(last, 0, split)
        soft_max(last, split, ROWS)
        soft_recip(last, 0, split)
        soft_sub(last, split, ROWS)
        soft_mul(last, 0, split)
        soft_exp(last, split, ROWS)
        store(last, 0, split)
        soft_sum(last, split, ROWS)
        soft_recip(last, split, ROWS)
        soft_mul(last, split, ROWS)
        store(last, split, ROWS)
